import numpy as np
import ml_dtypes


def mxq(x, axis, fmt="e4m3"):
    dtype, down = {"e4m3": (ml_dtypes.float8_e4m3fn, 7), "e5m2": (ml_dtypes.float8_e5m2, 14)}[fmt]
    v = np.moveaxis(np.asarray(x, np.float32).astype(ml_dtypes.bfloat16).astype(np.float64), axis, -1)
    blocks = v.reshape(v.shape[:-1] + (-1, 32))
    amax = np.abs(blocks).max(-1, keepdims=True)
    byte = np.maximum(np.where(amax > 0, np.frexp(amax)[1] - 1 + 127, 0) - down, 1)
    scale = np.exp2(byte - 127.0)
    codes = (blocks / scale).astype(np.float32).astype(dtype).astype(np.float64)
    return np.moveaxis((codes * scale).reshape(v.shape), -1, axis)


WIDE = False


def mx_kscale(k):
    if not WIDE:
        return np.ones(k)
    levels = np.array([10, -10, 5, -5, 0])
    a = np.random.permutation(np.resize(levels, k // 512 * 4)).reshape(k // 512, 4)
    idx = np.arange(k)
    return np.exp2(a[idx // 512, idx % 128 // 32])


BF16 = ml_dtypes.bfloat16


def bf(x):
    return np.asarray(x, np.float32).astype(BF16)


def f64(x):
    return np.asarray(x).astype(np.float64)


B, C, W, H, O = 128, 64, 32, 32, 512
K = C * W * H
G = np.sqrt(W * H)
SLO, SHI = 1.0 + 0.03 * G, 2.0 + 0.25 * G


def setup_inputs():
    t = mx_kscale(K).reshape(C, W * H)[np.arange(C), np.arange(C) * (W * H) // C].reshape(1, C, 1, 1)
    return {"x": bf(np.random.standard_normal((B, C, W, H)) * t),
            "cx": bf(np.random.uniform(-W / 2.0, W / 2.0, (O, 1, 1, 1))),
            "cy": bf(np.random.uniform(-H / 2.0, H / 2.0, (O, 1, 1, 1))),
            "sigma": bf(np.random.uniform(SLO, SHI, (O, 1, 1, 1))),
            "features": bf(np.random.standard_normal((O, C, 1, 1)) * 2.0 / (np.sqrt(C) * (SLO + SHI)) / t),
            "bias": bf(np.random.standard_normal(O))}


def reference(x, cx, cy, sigma, features, bias):
    x, cx, cy, sigma, features, bias = f64(x), f64(cx), f64(cy), f64(sigma), f64(features), f64(bias)
    w_edge = (W - 1) / 2.0
    h_edge = (H - 1) / 2.0
    grid_x = np.linspace(-w_edge, w_edge, W).reshape(1, 1, W, 1)
    grid_y = np.linspace(-h_edge, h_edge, H).reshape(1, 1, 1, H)
    d = (cx - grid_x) ** 2 + (cy - grid_y) ** 2
    spatial = np.exp(-d / sigma ** 2)
    weight = (spatial * features).reshape(O, K)
    return (mxq(x.reshape(B, K), 1, "e4m3") @ mxq(weight, 1, "e4m3").T) + bias

@@ -1,0 +1,299 @@
+from contextlib import ExitStack
+
+import concourse.mybir as mybir
+from concourse.masks import make_identity
+
+F32 = mybir.dt.float32
+BF16 = mybir.dt.bfloat16
+I32 = mybir.dt.int32
+U32 = mybir.dt.uint32
+U8 = mybir.dt.uint8
+FP8X4 = mybir.dt.float8_e4m3fn_x4
+ALU = mybir.AluOpType
+ACT = mybir.ActivationFunctionType
+
+P = 128
+BATCH, CHANNELS, OUTS = 128, 64, 512
+SPACE = 1024
+FLOPS = 2 * BATCH * OUTS * CHANNELS * SPACE
+
+GROUPS = 16
+QUADS = 4
+STEPS = CHANNELS * QUADS
+X_LEAD = 8
+X_CHUNK = 4
+N_SCALAR = 150
+MX_BUNCH = 2
+
+
+def scalar_share(step):
+    return ((step + 1) * N_SCALAR) // STEPS - (step * N_SCALAR) // STEPS
+
+
+def tile_gaussianspatialxfeaturelinear_kernel(tc, x, cx, cy, sigma, features, bias, out):
+    nc = tc.nc
+    x_flat = x.rearrange("b c w h -> b (c w h)")
+    with ExitStack() as ctx:
+        const = ctx.enter_context(tc.tile_pool(name="const", bufs=1))
+        arg_pool = ctx.enter_context(tc.tile_pool(name="arg", bufs=4))
+        x_pool = ctx.enter_context(tc.tile_pool(name="x", bufs=4))
+        prod_pool = ctx.enter_context(tc.tile_pool(name="prod", bufs=10))
+        w_pool = ctx.enter_context(tc.tile_pool(name="w", bufs=8))
+        xg_pool = ctx.enter_context(tc.tile_pool(name="xg", bufs=2))
+        xq_pool = ctx.enter_context(tc.tile_pool(name="xq", bufs=4))
+        ring = ctx.enter_context(tc.psum_pool(name="ring", bufs=7))
+        acc_pool = ctx.enter_context(tc.psum_pool(name="acc", bufs=1))
+        ctx.enter_context(tc.manual_schedule())
+
+        part_i = const.tile([P, 1], I32)
+        grid_i = const.tile([P, 2, 16], I32)
+        ident_bf = const.tile([P, P], BF16)
+        ident_f = const.tile([P, P], F32)
+        nc.gpsimd.iota(part_i[:], pattern=[[0, 1]], base=0, channel_multiplier=1)
+        nc.gpsimd.iota(grid_i[:, 0, :], pattern=[[16, 2], [1, 8]], base=0, channel_multiplier=0)
+        nc.gpsimd.iota(grid_i[:, 1, :], pattern=[[2, 16]], base=0, channel_multiplier=0)
+        make_identity(nc, ident_bf[:])
+        make_identity(nc, ident_f[:])
+
+        raw = const.tile([P, 64 + GROUPS * CHANNELS], BF16)
+        raw_i = raw[:].bitcast(I32)
+        nc.vector.memset(raw_i[32:64, :], 0)
+        nc.vector.memset(raw_i[64:128, :], 0)
+        nc.vector.memset(raw_i[0:32, 24:32], 0)
+        nc.sync.dma_start(out=raw[0:32, 0:16], in_=cx.rearrange("(l g) a b c -> l (g a b c)", g=GROUPS))
+        nc.sync.dma_start(out=raw[0:32, 16:32], in_=cy.rearrange("(l g) a b c -> l (g a b c)", g=GROUPS))
+        nc.sync.dma_start(out=raw[0:32, 32:48], in_=sigma.rearrange("(l g) a b c -> l (g a b c)", g=GROUPS))
+        nc.sync.dma_start(out=raw[0:32, 64:], in_=features.rearrange("(l g) c a b -> l (g c a b)", g=GROUPS))
+
+        x_tiles = {}
+
+        def x_load(j):
+            x_sb = x_pool.tile([P, X_CHUNK * SPACE], BF16)
+            nc.sync.dma_start(out=x_sb[:], in_=x_flat[:, j * X_CHUNK * SPACE : (j + 1) * X_CHUNK * SPACE])
+            x_tiles[j] = x_sb
+
+        for j in range(4):
+            x_load(j)
+        bias_sb = const.tile([P, OUTS], BF16)
+        nc.sync.dma_start(out=bias_sb[:], in_=bias.partition_broadcast(P))
+
+        warm = const.tile([P, 1], F32)
+        nc.vector.memset(warm[:], 0.0)
+        nc.scalar.activation(out=warm[:], in_=warm[:], func=ACT.Exp)
+
+        bit_i = const.tile([P, 2], I32)
+        nc.vector.tensor_scalar(
+            out=bit_i[:, 0:1], in0=part_i[:], scalar1=1, scalar2=1, op0=ALU.logical_shift_right, op1=ALU.bitwise_and
+        )
+        nc.vector.tensor_scalar(out=bit_i[:, 1:2], in0=part_i[:], scalar1=1, scalar2=None, op0=ALU.bitwise_and)
+        off = const.tile([P, 2], F32)
+        nc.vector.tensor_scalar(
+            out=off[:, 0:1], in0=bit_i[:, 0:1], scalar1=-8.0, scalar2=15.5, op0=ALU.mult, op1=ALU.add
+        )
+        nc.vector.tensor_scalar(
+            out=off[:, 1:2], in0=bit_i[:, 1:2], scalar1=-1.0, scalar2=15.5, op0=ALU.mult, op1=ALU.add
+        )
+        grid = const.tile([P, 2, 16], F32)
+        nc.vector.tensor_copy(out=grid[:], in_=grid_i[:])
+        spread = const.tile([P, 32, 4], BF16)
+        nc.vector.tensor_copy(out=spread[:], in_=ident_bf[:, 0:32].unsqueeze(2).to_broadcast([P, 32, 4]))
+        spread_flat = spread[:].rearrange("p l t -> p (l t)")
+
+        par_ps = ring.tile([P, 64], F32, tag="bank")
+        nc.tensor.matmul(out=par_ps[:], lhsT=spread_flat, rhs=raw[:, 0:64], start=True, stop=True)
+        par = const.tile([P, 4, 16], F32)
+        nc.vector.tensor_copy(out=par[:].rearrange("p v g -> p (v g)"), in_=par_ps[:])
+        feat = const.tile([P, GROUPS, CHANNELS], F32)
+        feat_flat = feat[:].rearrange("p g c -> p (g c)")
+        for h in range(2):
+            feat_ps = ring.tile([P, 512], F32, tag="bank")
+            nc.tensor.matmul(
+                out=feat_ps[:], lhsT=spread_flat, rhs=raw[:, 64 + 512 * h : 576 + 512 * h], start=True, stop=True
+            )
+            nc.scalar.copy(out=feat_flat[:, 512 * h : 512 * (h + 1)], in_=feat_ps[:])
+
+        x_banks = {}
+        xg_tiles = {}
+        xq_tiles = {}
+
+        def x_transposes(c):
+            words = x_tiles[c // X_CHUNK][:].bitcast(F32)
+            x_ps = ring.tile([P, 512], F32, tag="bank")
+            for v in range(4):
+                col = (c % X_CHUNK) * 512 + v * P
+                nc.tensor.transpose(out=x_ps[:, v * P : (v + 1) * P], in_=words[:, col : col + P], identity=ident_f[:])
+            x_banks[c] = x_ps
+
+        def x_evacuate(c):
+            if c % X_CHUNK == 0:
+                xg = xg_pool.tile([P, X_CHUNK * SPACE], BF16, align_bytes=64)
+                xg_tiles[c // X_CHUNK] = xg
+            dst = xg_tiles[c // X_CHUNK][:].bitcast(F32).rearrange(
+                "p (c g b u) -> p c g b u", c=X_CHUNK, g=2, b=BATCH, u=2
+            )
+            nc.scalar.copy(
+                out=dst[:, c % X_CHUNK], in_=x_banks[c][:].rearrange("p (g u b) -> p g b u", g=2, u=2, b=BATCH)
+            )
+
+        def x_quantise(j):
+            x_codes = xq_pool.tile([P, X_CHUNK * 2 * BATCH], U32, align_bytes=64)
+            x_scales = xq_pool.tile([P, X_CHUNK * 2 * BATCH], U8, align_bytes=64)
+            nc.vector.quantize_mx(out=x_codes[:].bitcast(FP8X4), scales=x_scales[:], in_=xg_tiles[j][:])
+            xq_tiles[j] = (x_codes, x_scales)
+
+        for c in range(4):
+            x_transposes(c)
+            x_evacuate(c)
+        x_load(4)
+
+        ctr = const.tile([P, 2, 16], F32)
+        for v in range(2):
+            nc.vector.tensor_scalar(
+                out=ctr[:, v, :], in0=par[:, v, :], scalar1=off[:, v : v + 1], scalar2=None, op0=ALU.add
+            )
+        inv = const.tile([P, 16], F32)
+        nc.vector.tensor_tensor(out=inv[:], in0=par[:, 2, :], in1=par[:, 2, :], op=ALU.mult)
+        nc.vector.reciprocal(out=inv[:], in_=inv[:])
+        dist = const.tile([P, 2, GROUPS, 16], F32)
+        full = [P, 2, GROUPS, 16]
+        nc.vector.tensor_tensor(
+            out=dist[:],
+            in0=ctr[:].unsqueeze(3).to_broadcast(full),
+            in1=grid[:].unsqueeze(2).to_broadcast(full),
+            op=ALU.subtract,
+        )
+        nc.vector.tensor_tensor(out=dist[:], in0=dist[:], in1=dist[:], op=ALU.mult)
+        nc.vector.tensor_tensor(
+            out=dist[:], in0=dist[:], in1=inv[:].unsqueeze(1).unsqueeze(3).to_broadcast(full), op=ALU.mult
+        )
+        gauss = []
+        for q in range(QUADS):
+            arg = arg_pool.tile([P, 4, 16, 16], F32)
+            nc.vector.tensor_tensor(
+                out=arg[:],
+                in0=dist[:, 0, 4 * q : 4 * q + 4, :].unsqueeze(3).to_broadcast([P, 4, 16, 16]),
+                in1=dist[:, 1, 4 * q : 4 * q + 4, :].unsqueeze(2).to_broadcast([P, 4, 16, 16]),
+                op=ALU.add,
+            )
+            gauss_q = const.tile([P, 4, 256], F32, name="gauss%d" % q)
+            nc.scalar.activation(
+                out=gauss_q[:].rearrange("p a k -> p (a k)"),
+                in_=arg[:].rearrange("p a i j -> p (a i j)"),
+                func=ACT.Exp,
+                scale=-1.0,
+            )
+            gauss.append(gauss_q)
+
+        for c in range(4, X_LEAD):
+            x_transposes(c)
+            x_evacuate(c)
+        x_load(5)
+
+        prods = {}
+        w_banks = {}
+        wg_tiles = {}
+        wq_tiles = {}
+        acc = acc_pool.tile([P, OUTS], F32)
+
+        def product_tile(step):
+            if step not in prods:
+                prod = prod_pool.tile([P, 4, 256], BF16)
+                prods[step] = prod
+            return prods[step]
+
+        def products(step, on_scalar):
+            c, q = divmod(step, QUADS)
+            n_scalar = scalar_share(step)
+            prod = product_tile(step)
+            for a in range(4):
+                scale = feat[:, 4 * q + a, c : c + 1]
+                if on_scalar and a >= 4 - n_scalar:
+                    nc.scalar.activation(out=prod[:, a, :], in_=gauss[q][:, a, :], func=ACT.Copy, scale=scale)
+                if not on_scalar and a < 4 - n_scalar:
+                    nc.vector.tensor_scalar(
+                        out=prod[:, a, :], in0=gauss[q][:, a, :], scalar1=scale, scalar2=None, op0=ALU.mult
+                    )
+
+        def w_transposes(step):
+            for g in range(2):
+                w_ps = ring.tile([P, 512], BF16, tag="bank")
+                for a in range(4):
+                    nc.tensor.transpose(
+                        out=w_ps[:, a * P : (a + 1) * P],
+                        in_=prods[step][:, a, g * P : (g + 1) * P],
+                        identity=ident_bf[:],
+                    )
+                w_banks[(step, g)] = w_ps
+
+        def w_evacuate(step):
+            c, q = divmod(step, QUADS)
+            for g in range(2):
+                if q == 0:
+                    wg = w_pool.tile([P, 4 * OUTS], BF16, align_bytes=64)
+                    wg_tiles[(c, g)] = wg
+                nc.scalar.copy(out=wg_tiles[(c, g)][:, 512 * q : 512 * (q + 1)], in_=w_banks[(step, g)][:])
+
+        def w_quantise(c, g):
+            w_codes = w_pool.tile([P, OUTS], U32, align_bytes=64)
+            w_scales = w_pool.tile([P, OUTS], U8, align_bytes=64)
+            nc.vector.quantize_mx(out=w_codes[:].bitcast(FP8X4), scales=w_scales[:], in_=wg_tiles[(c, g)][:])
+            wq_tiles[(c, g)] = (w_codes, w_scales)
+
+        def mx_pass(c, g):
+            x_codes, x_scales = xq_tiles[c // X_CHUNK]
+            w_codes, w_scales = wq_tiles[(c, g)]
+            cols = slice(((c % X_CHUNK) * 2 + g) * BATCH, ((c % X_CHUNK) * 2 + g + 1) * BATCH)
+            nc.tensor.matmul_mx(
+                out=acc[:],
+                lhsT=x_codes[:, cols].bitcast(FP8X4),
+                lhsT_scale=x_scales[:, cols],
+                rhs=w_codes[:].bitcast(FP8X4),
+                rhs_scale=w_scales[:],
+                start=(c == 0 and g == 0),
+                stop=(c == CHANNELS - 1 and g == 1),
+            )
+
+        products(0, True)
+        for tick in range(STEPS + 16):
+            if tick + 1 < STEPS:
+                products(tick + 1, True)
+            if tick < STEPS:
+                products(tick, False)
+            step = tick - 1
+            if 0 <= step < STEPS:
+                w_transposes(step)
+                c = step // QUADS + X_LEAD
+                if step % QUADS == 3 and c < CHANNELS:
+                    x_transposes(c)
+                    if c % X_CHUNK == 3 and c // X_CHUNK + 4 < CHANNELS // X_CHUNK:
+                        x_load(c // X_CHUNK + 4)
+            step = tick - 2
+            if 0 <= step < STEPS:
+                w_evacuate(step)
+                c = step // QUADS + X_LEAD
+                if step % QUADS == 3 and c < CHANNELS:
+                    x_evacuate(c)
+            for g in range(2):
+                c, rest = divmod(tick - 7 - 2 * g, QUADS)
+                if rest == 0 and 0 <= c < CHANNELS:
+                    w_quantise(c, g)
+            if tick % QUADS == 0:
+                for j in range(CHANNELS // X_CHUNK):
+                    last = X_CHUNK * j + 3
+                    when = QUADS * (last - X_LEAD) + 8 if last >= X_LEAD else QUADS * (j + 1)
+                    if when == tick:
+                        x_quantise(j)
+            c, rest = divmod(tick - 11, QUADS)
+            if rest == 0 and 0 <= c < CHANNELS and c % MX_BUNCH == MX_BUNCH - 1:
+                for cc in range(c - MX_BUNCH + 1, c + 1):
+                    for g in range(2):
+                        mx_pass(cc, g)
+
+        res = const.tile([P, OUTS], F32)
+        nc.vector.tensor_tensor(
+            out=res[:].rearrange("b (l g) -> b l g", g=GROUPS),
+            in0=acc[:].rearrange("b (g l) -> b l g", g=GROUPS),
+            in1=bias_sb[:].rearrange("b (l g) -> b l g", g=GROUPS),
+            op=ALU.add,
+        )
+        nc.sync.dma_start(out=out, in_=res[:])

@@ -38,7 +38,7 @@ def tile_gaussianspatialxfeaturelinear_kernel(tc, x, cx, cy, sigma, features, bi
         arg_pool = ctx.enter_context(tc.tile_pool(name="arg", bufs=4))
         x_pool = ctx.enter_context(tc.tile_pool(name="x", bufs=4))
         prod_pool = ctx.enter_context(tc.tile_pool(name="prod", bufs=10))
-        w_pool = ctx.enter_context(tc.tile_pool(name="w", bufs=8))
+        w_pool = ctx.enter_context(tc.tile_pool(name="w", bufs=4))
         xg_pool = ctx.enter_context(tc.tile_pool(name="xg", bufs=2))
         xq_pool = ctx.enter_context(tc.tile_pool(name="xq", bufs=4))
         ring = ctx.enter_context(tc.psum_pool(name="ring", bufs=7))
@@ -215,40 +215,42 @@ def tile_gaussianspatialxfeaturelinear_kernel(tc, x, cx, cy, sigma, features, bi
                     )
 
         def w_transposes(step):
+            w_ps = ring.tile([P, 2, 4, P], BF16, tag="bank")
             for g in range(2):
-                w_ps = ring.tile([P, 512], BF16, tag="bank")
                 for a in range(4):
                     nc.tensor.transpose(
-                        out=w_ps[:, a * P : (a + 1) * P],
-                        in_=prods[step][:, a, g * P : (g + 1) * P],
-                        identity=ident_bf[:],
+                        out=w_ps[:, g, a, :], in_=prods[step][:, a, g * P : (g + 1) * P], identity=ident_bf[:]
                     )
-                w_banks[(step, g)] = w_ps
+            w_banks[step] = w_ps
 
         def w_evacuate(step):
             c, q = divmod(step, QUADS)
-            for g in range(2):
-                if q == 0:
-                    wg = w_pool.tile([P, 4 * OUTS], BF16, align_bytes=64)
-                    wg_tiles[(c, g)] = wg
-                nc.scalar.copy(out=wg_tiles[(c, g)][:, 512 * q : 512 * (q + 1)], in_=w_banks[(step, g)][:])
+            if q == 0:
+                wg = w_pool.tile([P, 2, 4 * OUTS], BF16, align_bytes=64)
+                wg_tiles[c] = wg
+            nc.scalar.copy(
+                out=wg_tiles[c][:, :, 512 * q : 512 * (q + 1)], in_=w_banks[step][:].rearrange("p g a r -> p g (a r)")
+            )
 
-        def w_quantise(c, g):
-            w_codes = w_pool.tile([P, OUTS], U32, align_bytes=64)
-            w_scales = w_pool.tile([P, OUTS], U8, align_bytes=64)
-            nc.vector.quantize_mx(out=w_codes[:].bitcast(FP8X4), scales=w_scales[:], in_=wg_tiles[(c, g)][:])
-            wq_tiles[(c, g)] = (w_codes, w_scales)
+        def w_quantise(c):
+            w_codes = w_pool.tile([P, 2 * OUTS], U32, align_bytes=64)
+            w_scales = w_pool.tile([P, 2 * OUTS], U8, align_bytes=64)
+            nc.vector.quantize_mx(
+                out=w_codes[:].bitcast(FP8X4), scales=w_scales[:], in_=wg_tiles[c][:].rearrange("p g n -> p (g n)")
+            )
+            wq_tiles[c] = (w_codes, w_scales)
 
         def mx_pass(c, g):
             x_codes, x_scales = xq_tiles[c // X_CHUNK]
-            w_codes, w_scales = wq_tiles[(c, g)]
+            w_codes, w_scales = wq_tiles[c]
             cols = slice(((c % X_CHUNK) * 2 + g) * BATCH, ((c % X_CHUNK) * 2 + g + 1) * BATCH)
+            half = slice(g * OUTS, (g + 1) * OUTS)
             nc.tensor.matmul_mx(
                 out=acc[:],
                 lhsT=x_codes[:, cols].bitcast(FP8X4),
                 lhsT_scale=x_scales[:, cols],
-                rhs=w_codes[:].bitcast(FP8X4),
-                rhs_scale=w_scales[:],
+                rhs=w_codes[:, half].bitcast(FP8X4),
+                rhs_scale=w_scales[:, half],
                 start=(c == 0 and g == 0),
                 stop=(c == CHANNELS - 1 and g == 1),
             )
@@ -273,10 +275,9 @@ def tile_gaussianspatialxfeaturelinear_kernel(tc, x, cx, cy, sigma, features, bi
                 c = step // QUADS + X_LEAD
                 if step % QUADS == 3 and c < CHANNELS:
                     x_evacuate(c)
-            for g in range(2):
-                c, rest = divmod(tick - 7 - 2 * g, QUADS)
-                if rest == 0 and 0 <= c < CHANNELS:
-                    w_quantise(c, g)
+            c, rest = divmod(tick - 7, QUADS)
+            if rest == 0 and 0 <= c < CHANNELS:
+                w_quantise(c)
             if tick % QUADS == 0:
                 for j in range(CHANNELS // X_CHUNK):
                     last = X_CHUNK * j + 3

@@ -23,7 +23,8 @@ STEPS = CHANNELS * QUADS
 X_LEAD = 8
 X_CHUNK = 4
 N_SCALAR = 150
-MX_BUNCH = 2
+KICK_EVERY = 16
+KICK_PASSES = 2
 
 
 def scalar_share(step):
@@ -38,10 +39,11 @@ def tile_gaussianspatialxfeaturelinear_kernel(tc, x, cx, cy, sigma, features, bi
         arg_pool = ctx.enter_context(tc.tile_pool(name="arg", bufs=4))
         x_pool = ctx.enter_context(tc.tile_pool(name="x", bufs=4))
         prod_pool = ctx.enter_context(tc.tile_pool(name="prod", bufs=10))
-        w_pool = ctx.enter_context(tc.tile_pool(name="w", bufs=4))
+        w_pool = ctx.enter_context(tc.tile_pool(name="w", bufs=8))
         xg_pool = ctx.enter_context(tc.tile_pool(name="xg", bufs=2))
         xq_pool = ctx.enter_context(tc.tile_pool(name="xq", bufs=4))
-        ring = ctx.enter_context(tc.psum_pool(name="ring", bufs=7))
+        ring = ctx.enter_context(tc.psum_pool(name="ring", bufs=6))
+        idle_pool = ctx.enter_context(tc.psum_pool(name="idle", bufs=1))
         acc_pool = ctx.enter_context(tc.psum_pool(name="acc", bufs=1))
         ctx.enter_context(tc.manual_schedule())
 
@@ -135,11 +137,19 @@ def tile_gaussianspatialxfeaturelinear_kernel(tc, x, cx, cy, sigma, features, bi
                 out=dst[:, c % X_CHUNK], in_=x_banks[c][:].rearrange("p (g u b) -> p g b u", g=2, u=2, b=BATCH)
             )
 
-        def x_quantise(j):
-            x_codes = xq_pool.tile([P, X_CHUNK * 2 * BATCH], U32, align_bytes=64)
-            x_scales = xq_pool.tile([P, X_CHUNK * 2 * BATCH], U8, align_bytes=64)
-            nc.vector.quantize_mx(out=x_codes[:].bitcast(FP8X4), scales=x_scales[:], in_=xg_tiles[j][:])
-            xq_tiles[j] = (x_codes, x_scales)
+        def x_quantise(c):
+            j, i = divmod(c, X_CHUNK)
+            if i == 0:
+                x_codes = xq_pool.tile([P, X_CHUNK * 2 * BATCH], U32, align_bytes=64)
+                x_scales = xq_pool.tile([P, X_CHUNK * 2 * BATCH], U8, align_bytes=64)
+                xq_tiles[j] = (x_codes, x_scales)
+            codes, scales = xq_tiles[j]
+            words = slice(i * 2 * BATCH, (i + 1) * 2 * BATCH)
+            nc.vector.quantize_mx(
+                out=codes[:, words].bitcast(FP8X4),
+                scales=scales[:, words],
+                in_=xg_tiles[j][:, i * SPACE : (i + 1) * SPACE],
+            )
 
         for c in range(4):
             x_transposes(c)
@@ -215,53 +225,77 @@ def tile_gaussianspatialxfeaturelinear_kernel(tc, x, cx, cy, sigma, features, bi
                     )
 
         def w_transposes(step):
-            w_ps = ring.tile([P, 2, 4, P], BF16, tag="bank")
             for g in range(2):
+                w_ps = ring.tile([P, 512], BF16, tag="bank")
                 for a in range(4):
                     nc.tensor.transpose(
-                        out=w_ps[:, g, a, :], in_=prods[step][:, a, g * P : (g + 1) * P], identity=ident_bf[:]
+                        out=w_ps[:, a * P : (a + 1) * P],
+                        in_=prods[step][:, a, g * P : (g + 1) * P],
+                        identity=ident_bf[:],
                     )
-            w_banks[step] = w_ps
+                w_banks[(step, g)] = w_ps
 
         def w_evacuate(step):
             c, q = divmod(step, QUADS)
-            if q == 0:
-                wg = w_pool.tile([P, 2, 4 * OUTS], BF16, align_bytes=64)
-                wg_tiles[c] = wg
-            nc.scalar.copy(
-                out=wg_tiles[c][:, :, 512 * q : 512 * (q + 1)], in_=w_banks[step][:].rearrange("p g a r -> p g (a r)")
-            )
+            for g in range(2):
+                if q == 0:
+                    wg = w_pool.tile([P, 4 * OUTS], BF16, align_bytes=64)
+                    wg_tiles[(c, g)] = wg
+                nc.scalar.copy(out=wg_tiles[(c, g)][:, 512 * q : 512 * (q + 1)], in_=w_banks[(step, g)][:])
 
-        def w_quantise(c):
-            w_codes = w_pool.tile([P, 2 * OUTS], U32, align_bytes=64)
-            w_scales = w_pool.tile([P, 2 * OUTS], U8, align_bytes=64)
+        def w_quantise(c, g, h):
+            if h == 0:
+                w_codes = w_pool.tile([P, OUTS], U32, align_bytes=64)
+                w_scales = w_pool.tile([P, OUTS], U8, align_bytes=64)
+                wq_tiles[(c, g)] = (w_codes, w_scales)
+            codes, scales = wq_tiles[(c, g)]
+            words = slice(h * 256, (h + 1) * 256)
             nc.vector.quantize_mx(
-                out=w_codes[:].bitcast(FP8X4), scales=w_scales[:], in_=wg_tiles[c][:].rearrange("p g n -> p (g n)")
+                out=codes[:, words].bitcast(FP8X4),
+                scales=scales[:, words],
+                in_=wg_tiles[(c, g)][:, h * 1024 : (h + 1) * 1024],
             )
-            wq_tiles[c] = (w_codes, w_scales)
 
         def mx_pass(c, g):
             x_codes, x_scales = xq_tiles[c // X_CHUNK]
-            w_codes, w_scales = wq_tiles[c]
+            w_codes, w_scales = wq_tiles[(c, g)]
             cols = slice(((c % X_CHUNK) * 2 + g) * BATCH, ((c % X_CHUNK) * 2 + g + 1) * BATCH)
-            half = slice(g * OUTS, (g + 1) * OUTS)
             nc.tensor.matmul_mx(
                 out=acc[:],
                 lhsT=x_codes[:, cols].bitcast(FP8X4),
                 lhsT_scale=x_scales[:, cols],
-                rhs=w_codes[:, half].bitcast(FP8X4),
-                rhs_scale=w_scales[:, half],
+                rhs=w_codes[:].bitcast(FP8X4),
+                rhs_scale=w_scales[:],
                 start=(c == 0 and g == 0),
                 stop=(c == CHANNELS - 1 and g == 1),
             )
 
+        idle = idle_pool.tile([P, OUTS], F32)
+
+        def idle_pass(stationary, moving):
+            nc.tensor.matmul_mx(
+                out=idle[:],
+                lhsT=stationary[0][:, 0:BATCH].bitcast(FP8X4),
+                lhsT_scale=stationary[1][:, 0:BATCH],
+                rhs=moving[0][:, 0:OUTS].bitcast(FP8X4),
+                rhs_scale=moving[1][:, 0:OUTS],
+                start=True,
+                stop=True,
+            )
+
         products(0, True)
+        n_passes = 0
         for tick in range(STEPS + 16):
             if tick + 1 < STEPS:
                 products(tick + 1, True)
             if tick < STEPS:
                 products(tick, False)
+            if tick < X_LEAD:
+                x_quantise(tick)
             step = tick - 1
+            if step == 0:
+                for i in range(3):
+                    idle_pass(xq_tiles[0], xq_tiles[0])
             if 0 <= step < STEPS:
                 w_transposes(step)
                 c = step // QUADS + X_LEAD
@@ -275,20 +309,22 @@ def tile_gaussianspatialxfeaturelinear_kernel(tc, x, cx, cy, sigma, features, bi
                 c = step // QUADS + X_LEAD
                 if step % QUADS == 3 and c < CHANNELS:
                     x_evacuate(c)
-            c, rest = divmod(tick - 7, QUADS)
-            if rest == 0 and 0 <= c < CHANNELS:
-                w_quantise(c)
-            if tick % QUADS == 0:
-                for j in range(CHANNELS // X_CHUNK):
-                    last = X_CHUNK * j + 3
-                    when = QUADS * (last - X_LEAD) + 8 if last >= X_LEAD else QUADS * (j + 1)
-                    if when == tick:
-                        x_quantise(j)
-            c, rest = divmod(tick - 11, QUADS)
-            if rest == 0 and 0 <= c < CHANNELS and c % MX_BUNCH == MX_BUNCH - 1:
-                for cc in range(c - MX_BUNCH + 1, c + 1):
-                    for g in range(2):
-                        mx_pass(cc, g)
+            c, piece = divmod(tick - 5, QUADS)
+            if 0 <= c < CHANNELS:
+                w_quantise(c, piece % 2, piece // 2)
+            c, rest = divmod(tick - 8, QUADS)
+            if rest == 0 and c >= 0 and c + X_LEAD < CHANNELS:
+                x_quantise(c + X_LEAD)
+            c, rest = divmod(tick - 9, QUADS)
+            if rest % 2 == 0:
+                if 0 <= c < CHANNELS:
+                    mx_pass(c, rest // 2)
+                    n_passes += 1
+                    if n_passes % KICK_EVERY == 0:
+                        for i in range(KICK_PASSES):
+                            idle_pass(xq_tiles[c // X_CHUNK], wq_tiles[(c, rest // 2)])
+                elif c < 0 and tick >= 3:
+                    idle_pass(xq_tiles[0], xq_tiles[0])
 
         res = const.tile([P, OUTS], F32)
         nc.vector.tensor_tensor(

@@ -23,7 +23,7 @@ STEPS = CHANNELS * QUADS
 X_LEAD = 8
 X_CHUNK = 4
 N_SCALAR = 150
-KICK_EVERY = 16
+KICK_EVERY = 32
 KICK_PASSES = 2
 
 
@@ -298,16 +298,16 @@ def tile_gaussianspatialxfeaturelinear_kernel(tc, x, cx, cy, sigma, features, bi
                     idle_pass(xq_tiles[0], xq_tiles[0])
             if 0 <= step < STEPS:
                 w_transposes(step)
-                c = step // QUADS + X_LEAD
-                if step % QUADS == 3 and c < CHANNELS:
+                c = step // QUADS - 1 + X_LEAD
+                if step % QUADS == 0 and X_LEAD <= c < CHANNELS:
                     x_transposes(c)
                     if c % X_CHUNK == 3 and c // X_CHUNK + 4 < CHANNELS // X_CHUNK:
                         x_load(c // X_CHUNK + 4)
             step = tick - 2
             if 0 <= step < STEPS:
                 w_evacuate(step)
-                c = step // QUADS + X_LEAD
-                if step % QUADS == 3 and c < CHANNELS:
+                c = step // QUADS - 1 + X_LEAD
+                if step % QUADS == 0 and X_LEAD <= c < CHANNELS:
                     x_evacuate(c)
             c, piece = divmod(tick - 5, QUADS)
             if 0 <= c < CHANNELS:
@@ -320,7 +320,7 @@ def tile_gaussianspatialxfeaturelinear_kernel(tc, x, cx, cy, sigma, features, bi
                 if 0 <= c < CHANNELS:
                     mx_pass(c, rest // 2)
                     n_passes += 1
-                    if n_passes % KICK_EVERY == 0:
+                    if n_passes % KICK_EVERY == 0 and n_passes < 2 * CHANNELS:
                         for i in range(KICK_PASSES):
                             idle_pass(xq_tiles[c // X_CHUNK], wq_tiles[(c, rest // 2)])
                 elif c < 0 and tick >= 3:

@@ -22,7 +22,7 @@ QUADS = 4
 STEPS = CHANNELS * QUADS
 X_LEAD = 8
 X_CHUNK = 4
-N_SCALAR = 150
+N_SCALAR = 120
 KICK_EVERY = 32
 KICK_PASSES = 2
 

@@ -22,7 +22,7 @@ QUADS = 4
 STEPS = CHANNELS * QUADS
 X_LEAD = 8
 X_CHUNK = 4
-N_SCALAR = 120
+N_SCALAR = 185
 KICK_EVERY = 32
 KICK_PASSES = 2
 

@@ -22,7 +22,7 @@ QUADS = 4
 STEPS = CHANNELS * QUADS
 X_LEAD = 8
 X_CHUNK = 4
-N_SCALAR = 185
+N_SCALAR = 175
 KICK_EVERY = 32
 KICK_PASSES = 2
 
@@ -144,11 +144,11 @@ def tile_gaussianspatialxfeaturelinear_kernel(tc, x, cx, cy, sigma, features, bi
                 x_scales = xq_pool.tile([P, X_CHUNK * 2 * BATCH], U8, align_bytes=64)
                 xq_tiles[j] = (x_codes, x_scales)
             codes, scales = xq_tiles[j]
-            words = slice(i * 2 * BATCH, (i + 1) * 2 * BATCH)
+            words = slice(i * 2 * BATCH, (i + 2) * 2 * BATCH)
             nc.vector.quantize_mx(
                 out=codes[:, words].bitcast(FP8X4),
                 scales=scales[:, words],
-                in_=xg_tiles[j][:, i * SPACE : (i + 1) * SPACE],
+                in_=xg_tiles[j][:, i * SPACE : (i + 2) * SPACE],
             )
 
         for c in range(4):
@@ -243,18 +243,11 @@ def tile_gaussianspatialxfeaturelinear_kernel(tc, x, cx, cy, sigma, features, bi
                     wg_tiles[(c, g)] = wg
                 nc.scalar.copy(out=wg_tiles[(c, g)][:, 512 * q : 512 * (q + 1)], in_=w_banks[(step, g)][:])
 
-        def w_quantise(c, g, h):
-            if h == 0:
-                w_codes = w_pool.tile([P, OUTS], U32, align_bytes=64)
-                w_scales = w_pool.tile([P, OUTS], U8, align_bytes=64)
-                wq_tiles[(c, g)] = (w_codes, w_scales)
-            codes, scales = wq_tiles[(c, g)]
-            words = slice(h * 256, (h + 1) * 256)
-            nc.vector.quantize_mx(
-                out=codes[:, words].bitcast(FP8X4),
-                scales=scales[:, words],
-                in_=wg_tiles[(c, g)][:, h * 1024 : (h + 1) * 1024],
-            )
+        def w_quantise(c, g):
+            w_codes = w_pool.tile([P, OUTS], U32, align_bytes=64)
+            w_scales = w_pool.tile([P, OUTS], U8, align_bytes=64)
+            nc.vector.quantize_mx(out=w_codes[:].bitcast(FP8X4), scales=w_scales[:], in_=wg_tiles[(c, g)][:])
+            wq_tiles[(c, g)] = (w_codes, w_scales)
 
         def mx_pass(c, g):
             x_codes, x_scales = xq_tiles[c // X_CHUNK]
@@ -290,8 +283,8 @@ def tile_gaussianspatialxfeaturelinear_kernel(tc, x, cx, cy, sigma, features, bi
                 products(tick + 1, True)
             if tick < STEPS:
                 products(tick, False)
-            if tick < X_LEAD:
-                x_quantise(tick)
+            if tick < X_LEAD and tick % 2 == 1:
+                x_quantise(tick - 1)
             step = tick - 1
             if step == 0:
                 for i in range(3):
@@ -309,12 +302,12 @@ def tile_gaussianspatialxfeaturelinear_kernel(tc, x, cx, cy, sigma, features, bi
                 c = step // QUADS - 1 + X_LEAD
                 if step % QUADS == 0 and X_LEAD <= c < CHANNELS:
                     x_evacuate(c)
-            c, piece = divmod(tick - 5, QUADS)
-            if 0 <= c < CHANNELS:
-                w_quantise(c, piece % 2, piece // 2)
-            c, rest = divmod(tick - 8, QUADS)
-            if rest == 0 and c >= 0 and c + X_LEAD < CHANNELS:
-                x_quantise(c + X_LEAD)
+            c, rest = divmod(tick - 6, QUADS)
+            if rest % 2 == 0 and 0 <= c < CHANNELS:
+                w_quantise(c, rest // 2)
+            c, rest = divmod(tick - 11, 2 * QUADS)
+            if rest == 0 and c >= 0 and 2 * c + X_LEAD < CHANNELS:
+                x_quantise(2 * c + X_LEAD)
             c, rest = divmod(tick - 9, QUADS)
             if rest % 2 == 0:
                 if 0 <= c < CHANNELS:

@@ -17,12 +17,12 @@ BATCH, CHANNELS, OUTS = 128, 64, 512
 SPACE = 1024
 FLOPS = 2 * BATCH * OUTS * CHANNELS * SPACE
 
-GROUPS = 16
+GROUPS = 8
 QUADS = 4
 STEPS = CHANNELS * QUADS
 X_LEAD = 8
 X_CHUNK = 4
-N_SCALAR = 175
+N_SCALAR = 170
 KICK_EVERY = 32
 KICK_PASSES = 2
 
@@ -48,24 +48,24 @@ def tile_gaussianspatialxfeaturelinear_kernel(tc, x, cx, cy, sigma, features, bi
         ctx.enter_context(tc.manual_schedule())
 
         part_i = const.tile([P, 1], I32)
-        grid_i = const.tile([P, 2, 16], I32)
+        grid_i = const.tile([P, 48], I32)
         ident_bf = const.tile([P, P], BF16)
         ident_f = const.tile([P, P], F32)
         nc.gpsimd.iota(part_i[:], pattern=[[0, 1]], base=0, channel_multiplier=1)
-        nc.gpsimd.iota(grid_i[:, 0, :], pattern=[[16, 2], [1, 8]], base=0, channel_multiplier=0)
-        nc.gpsimd.iota(grid_i[:, 1, :], pattern=[[2, 16]], base=0, channel_multiplier=0)
+        nc.gpsimd.iota(grid_i[:, 0:32], pattern=[[1, 32]], base=0, channel_multiplier=0)
+        nc.gpsimd.iota(grid_i[:, 32:48], pattern=[[2, 16]], base=0, channel_multiplier=0)
         make_identity(nc, ident_bf[:])
         make_identity(nc, ident_f[:])
 
-        raw = const.tile([P, 64 + GROUPS * CHANNELS], BF16)
+        raw = const.tile([P, 64 + 16 * CHANNELS], BF16)
         raw_i = raw[:].bitcast(I32)
         nc.vector.memset(raw_i[32:64, :], 0)
         nc.vector.memset(raw_i[64:128, :], 0)
         nc.vector.memset(raw_i[0:32, 24:32], 0)
-        nc.sync.dma_start(out=raw[0:32, 0:16], in_=cx.rearrange("(l g) a b c -> l (g a b c)", g=GROUPS))
-        nc.sync.dma_start(out=raw[0:32, 16:32], in_=cy.rearrange("(l g) a b c -> l (g a b c)", g=GROUPS))
-        nc.sync.dma_start(out=raw[0:32, 32:48], in_=sigma.rearrange("(l g) a b c -> l (g a b c)", g=GROUPS))
-        nc.sync.dma_start(out=raw[0:32, 64:], in_=features.rearrange("(l g) c a b -> l (g c a b)", g=GROUPS))
+        nc.sync.dma_start(out=raw[0:32, 0:16], in_=cx.rearrange("(l g) a b c -> l (g a b c)", g=16))
+        nc.sync.dma_start(out=raw[0:32, 16:32], in_=cy.rearrange("(l g) a b c -> l (g a b c)", g=16))
+        nc.sync.dma_start(out=raw[0:32, 32:48], in_=sigma.rearrange("(l g) a b c -> l (g a b c)", g=16))
+        nc.sync.dma_start(out=raw[0:32, 64:], in_=features.rearrange("(l g) c a b -> l (g c a b)", g=16))
 
         x_tiles = {}
 
@@ -83,36 +83,37 @@ def tile_gaussianspatialxfeaturelinear_kernel(tc, x, cx, cy, sigma, features, bi
         nc.vector.memset(warm[:], 0.0)
         nc.scalar.activation(out=warm[:], in_=warm[:], func=ACT.Exp)
 
-        bit_i = const.tile([P, 2], I32)
-        nc.vector.tensor_scalar(
-            out=bit_i[:, 0:1], in0=part_i[:], scalar1=1, scalar2=1, op0=ALU.logical_shift_right, op1=ALU.bitwise_and
-        )
-        nc.vector.tensor_scalar(out=bit_i[:, 1:2], in0=part_i[:], scalar1=1, scalar2=None, op0=ALU.bitwise_and)
-        off = const.tile([P, 2], F32)
-        nc.vector.tensor_scalar(
-            out=off[:, 0:1], in0=bit_i[:, 0:1], scalar1=-8.0, scalar2=15.5, op0=ALU.mult, op1=ALU.add
-        )
-        nc.vector.tensor_scalar(
-            out=off[:, 1:2], in0=bit_i[:, 1:2], scalar1=-1.0, scalar2=15.5, op0=ALU.mult, op1=ALU.add
-        )
-        grid = const.tile([P, 2, 16], F32)
+        bit_i = const.tile([P, 1], I32)
+        nc.vector.tensor_scalar(out=bit_i[:], in0=part_i[:], scalar1=1, scalar2=None, op0=ALU.bitwise_and)
+        off = const.tile([P, 1], F32)
+        nc.vector.tensor_scalar(out=off[:], in0=bit_i[:], scalar1=-1.0, scalar2=15.5, op0=ALU.mult, op1=ALU.add)
+        grid = const.tile([P, 48], F32)
         nc.vector.tensor_copy(out=grid[:], in_=grid_i[:])
-        spread = const.tile([P, 32, 4], BF16)
-        nc.vector.tensor_copy(out=spread[:], in_=ident_bf[:, 0:32].unsqueeze(2).to_broadcast([P, 32, 4]))
-        spread_flat = spread[:].rearrange("p l t -> p (l t)")
+        spread = const.tile([P, 2, P], BF16)
+        nc.vector.memset(spread[:].rearrange("p h r -> p (h r)").bitcast(I32), 0)
+        for h in range(2):
+            nc.vector.tensor_copy(
+                out=spread[:, h, :].rearrange("p (l k e) -> p l k e", l=32, k=2, e=2)[:, :, h, :],
+                in_=ident_bf[:, 0:32].unsqueeze(2).to_broadcast([P, 32, 2]),
+            )
 
-        par_ps = ring.tile([P, 64], F32, tag="bank")
-        nc.tensor.matmul(out=par_ps[:], lhsT=spread_flat, rhs=raw[:, 0:64], start=True, stop=True)
-        par = const.tile([P, 4, 16], F32)
+        par_ps = ring.tile([P, 4 * GROUPS], F32, tag="bank")
+        feat_ps = ring.tile([P, 512], F32, tag="bank")
+        raw_par = raw[:, 0:64].rearrange("p (v k g) -> p v k g", v=4, k=2, g=GROUPS)
+        for h in range(2):
+            nc.tensor.matmul(out=par_ps[:], lhsT=spread[:, h, :], rhs=raw_par[:, :, h, :], start=(h == 0), stop=(h == 1))
+        for h in range(2):
+            nc.tensor.matmul(
+                out=feat_ps[:],
+                lhsT=spread[:, h, :],
+                rhs=raw[:, 64 + 512 * h : 576 + 512 * h],
+                start=(h == 0),
+                stop=(h == 1),
+            )
+        par = const.tile([P, 4, GROUPS], F32)
         nc.vector.tensor_copy(out=par[:].rearrange("p v g -> p (v g)"), in_=par_ps[:])
         feat = const.tile([P, GROUPS, CHANNELS], F32)
-        feat_flat = feat[:].rearrange("p g c -> p (g c)")
-        for h in range(2):
-            feat_ps = ring.tile([P, 512], F32, tag="bank")
-            nc.tensor.matmul(
-                out=feat_ps[:], lhsT=spread_flat, rhs=raw[:, 64 + 512 * h : 576 + 512 * h], start=True, stop=True
-            )
-            nc.scalar.copy(out=feat_flat[:, 512 * h : 512 * (h + 1)], in_=feat_ps[:])
+        nc.scalar.copy(out=feat[:].rearrange("p g c -> p (g c)"), in_=feat_ps[:])
 
         x_banks = {}
         xg_tiles = {}
@@ -144,11 +145,11 @@ def tile_gaussianspatialxfeaturelinear_kernel(tc, x, cx, cy, sigma, features, bi
                 x_scales = xq_pool.tile([P, X_CHUNK * 2 * BATCH], U8, align_bytes=64)
                 xq_tiles[j] = (x_codes, x_scales)
             codes, scales = xq_tiles[j]
-            words = slice(i * 2 * BATCH, (i + 2) * 2 * BATCH)
+            words = slice(i * 2 * BATCH, (i + 1) * 2 * BATCH)
             nc.vector.quantize_mx(
                 out=codes[:, words].bitcast(FP8X4),
                 scales=scales[:, words],
-                in_=xg_tiles[j][:, i * SPACE : (i + 2) * SPACE],
+                in_=xg_tiles[j][:, i * SPACE : (i + 1) * SPACE],
             )
 
         for c in range(4):
@@ -156,36 +157,39 @@ def tile_gaussianspatialxfeaturelinear_kernel(tc, x, cx, cy, sigma, features, bi
             x_evacuate(c)
         x_load(4)
 
-        ctr = const.tile([P, 2, 16], F32)
-        for v in range(2):
-            nc.vector.tensor_scalar(
-                out=ctr[:, v, :], in0=par[:, v, :], scalar1=off[:, v : v + 1], scalar2=None, op0=ALU.add
-            )
-        inv = const.tile([P, 16], F32)
+        ctr = const.tile([P, 2, GROUPS], F32)
+        nc.vector.tensor_scalar(out=ctr[:, 0, :], in0=par[:, 0, :], scalar1=15.5, scalar2=None, op0=ALU.add)
+        nc.vector.tensor_scalar(out=ctr[:, 1, :], in0=par[:, 1, :], scalar1=off[:], scalar2=None, op0=ALU.add)
+        inv = const.tile([P, GROUPS], F32)
         nc.vector.tensor_tensor(out=inv[:], in0=par[:, 2, :], in1=par[:, 2, :], op=ALU.mult)
         nc.vector.reciprocal(out=inv[:], in_=inv[:])
-        dist = const.tile([P, 2, GROUPS, 16], F32)
-        full = [P, 2, GROUPS, 16]
+        dist = const.tile([P, GROUPS, 48], F32)
         nc.vector.tensor_tensor(
-            out=dist[:],
-            in0=ctr[:].unsqueeze(3).to_broadcast(full),
-            in1=grid[:].unsqueeze(2).to_broadcast(full),
+            out=dist[:, :, 0:32],
+            in0=ctr[:, 0, :].unsqueeze(2).to_broadcast([P, GROUPS, 32]),
+            in1=grid[:, 0:32].unsqueeze(1).to_broadcast([P, GROUPS, 32]),
+            op=ALU.subtract,
+        )
+        nc.vector.tensor_tensor(
+            out=dist[:, :, 32:48],
+            in0=ctr[:, 1, :].unsqueeze(2).to_broadcast([P, GROUPS, 16]),
+            in1=grid[:, 32:48].unsqueeze(1).to_broadcast([P, GROUPS, 16]),
             op=ALU.subtract,
         )
         nc.vector.tensor_tensor(out=dist[:], in0=dist[:], in1=dist[:], op=ALU.mult)
         nc.vector.tensor_tensor(
-            out=dist[:], in0=dist[:], in1=inv[:].unsqueeze(1).unsqueeze(3).to_broadcast(full), op=ALU.mult
+            out=dist[:], in0=dist[:], in1=inv[:].unsqueeze(2).to_broadcast([P, GROUPS, 48]), op=ALU.mult
         )
         gauss = []
         for q in range(QUADS):
-            arg = arg_pool.tile([P, 4, 16, 16], F32)
+            arg = arg_pool.tile([P, 2, 32, 16], F32)
             nc.vector.tensor_tensor(
                 out=arg[:],
-                in0=dist[:, 0, 4 * q : 4 * q + 4, :].unsqueeze(3).to_broadcast([P, 4, 16, 16]),
-                in1=dist[:, 1, 4 * q : 4 * q + 4, :].unsqueeze(2).to_broadcast([P, 4, 16, 16]),
+                in0=dist[:, 2 * q : 2 * q + 2, 0:32].unsqueeze(3).to_broadcast([P, 2, 32, 16]),
+                in1=dist[:, 2 * q : 2 * q + 2, 32:48].unsqueeze(2).to_broadcast([P, 2, 32, 16]),
                 op=ALU.add,
             )
-            gauss_q = const.tile([P, 4, 256], F32, name="gauss%d" % q)
+            gauss_q = const.tile([P, 2, 512], F32, name="gauss%d" % q)
             nc.scalar.activation(
                 out=gauss_q[:].rearrange("p a k -> p (a k)"),
                 in_=arg[:].rearrange("p a i j -> p (a i j)"),
@@ -207,7 +211,7 @@ def tile_gaussianspatialxfeaturelinear_kernel(tc, x, cx, cy, sigma, features, bi
 
         def product_tile(step):
             if step not in prods:
-                prod = prod_pool.tile([P, 4, 256], BF16)
+                prod = prod_pool.tile([P, 2, 512], BF16)
                 prods[step] = prod
             return prods[step]
 
@@ -215,24 +219,29 @@ def tile_gaussianspatialxfeaturelinear_kernel(tc, x, cx, cy, sigma, features, bi
             c, q = divmod(step, QUADS)
             n_scalar = scalar_share(step)
             prod = product_tile(step)
-            for a in range(4):
-                scale = feat[:, 4 * q + a, c : c + 1]
-                if on_scalar and a >= 4 - n_scalar:
-                    nc.scalar.activation(out=prod[:, a, :], in_=gauss[q][:, a, :], func=ACT.Copy, scale=scale)
-                if not on_scalar and a < 4 - n_scalar:
+            for a in range(2):
+                scale = feat[:, 2 * q + a, c : c + 1]
+                shared = a == 1 and n_scalar == 1
+                if on_scalar and shared:
+                    nc.scalar.activation(
+                        out=prod[:, a, 256:512], in_=gauss[q][:, a, 256:512], func=ACT.Copy, scale=scale
+                    )
+                if not on_scalar:
+                    width = 256 if shared else 512
                     nc.vector.tensor_scalar(
-                        out=prod[:, a, :], in0=gauss[q][:, a, :], scalar1=scale, scalar2=None, op0=ALU.mult
+                        out=prod[:, a, 0:width], in0=gauss[q][:, a, 0:width], scalar1=scale, scalar2=None, op0=ALU.mult
                     )
 
         def w_transposes(step):
             for g in range(2):
-                w_ps = ring.tile([P, 512], BF16, tag="bank")
-                for a in range(4):
-                    nc.tensor.transpose(
-                        out=w_ps[:, a * P : (a + 1) * P],
-                        in_=prods[step][:, a, g * P : (g + 1) * P],
-                        identity=ident_bf[:],
-                    )
+                w_ps = ring.tile([P, 2, 64, 2, 2], BF16, tag="bank")
+                for a in range(2):
+                    for u in range(2):
+                        nc.tensor.transpose(
+                            out=w_ps[:, a, :, u, :],
+                            in_=prods[step][:, a, (2 * g + u) * P : (2 * g + u + 1) * P],
+                            identity=ident_bf[:],
+                        )
                 w_banks[(step, g)] = w_ps
 
         def w_evacuate(step):
@@ -241,13 +250,23 @@ def tile_gaussianspatialxfeaturelinear_kernel(tc, x, cx, cy, sigma, features, bi
                 if q == 0:
                     wg = w_pool.tile([P, 4 * OUTS], BF16, align_bytes=64)
                     wg_tiles[(c, g)] = wg
-                nc.scalar.copy(out=wg_tiles[(c, g)][:, 512 * q : 512 * (q + 1)], in_=w_banks[(step, g)][:])
+                nc.scalar.copy(
+                    out=wg_tiles[(c, g)][:, 512 * q : 512 * (q + 1)],
+                    in_=w_banks[(step, g)][:].rearrange("p a l u e -> p (a l u e)"),
+                )
 
-        def w_quantise(c, g):
-            w_codes = w_pool.tile([P, OUTS], U32, align_bytes=64)
-            w_scales = w_pool.tile([P, OUTS], U8, align_bytes=64)
-            nc.vector.quantize_mx(out=w_codes[:].bitcast(FP8X4), scales=w_scales[:], in_=wg_tiles[(c, g)][:])
-            wq_tiles[(c, g)] = (w_codes, w_scales)
+        def w_quantise(c, g, h):
+            if h == 0:
+                w_codes = w_pool.tile([P, OUTS], U32, align_bytes=64)
+                w_scales = w_pool.tile([P, OUTS], U8, align_bytes=64)
+                wq_tiles[(c, g)] = (w_codes, w_scales)
+            codes, scales = wq_tiles[(c, g)]
+            words = slice(h * 256, (h + 1) * 256)
+            nc.vector.quantize_mx(
+                out=codes[:, words].bitcast(FP8X4),
+                scales=scales[:, words],
+                in_=wg_tiles[(c, g)][:, h * 1024 : (h + 1) * 1024],
+            )
 
         def mx_pass(c, g):
             x_codes, x_scales = xq_tiles[c // X_CHUNK]
@@ -283,8 +302,8 @@ def tile_gaussianspatialxfeaturelinear_kernel(tc, x, cx, cy, sigma, features, bi
                 products(tick + 1, True)
             if tick < STEPS:
                 products(tick, False)
-            if tick < X_LEAD and tick % 2 == 1:
-                x_quantise(tick - 1)
+            if tick < X_LEAD:
+                x_quantise(tick)
             step = tick - 1
             if step == 0:
                 for i in range(3):
@@ -302,12 +321,12 @@ def tile_gaussianspatialxfeaturelinear_kernel(tc, x, cx, cy, sigma, features, bi
                 c = step // QUADS - 1 + X_LEAD
                 if step % QUADS == 0 and X_LEAD <= c < CHANNELS:
                     x_evacuate(c)
-            c, rest = divmod(tick - 6, QUADS)
-            if rest % 2 == 0 and 0 <= c < CHANNELS:
-                w_quantise(c, rest // 2)
-            c, rest = divmod(tick - 11, 2 * QUADS)
-            if rest == 0 and c >= 0 and 2 * c + X_LEAD < CHANNELS:
-                x_quantise(2 * c + X_LEAD)
+            c, piece = divmod(tick - 5, QUADS)
+            if 0 <= c < CHANNELS:
+                w_quantise(c, piece % 2, piece // 2)
+            c, rest = divmod(tick - 8, QUADS)
+            if rest == 0 and c >= 0 and c + X_LEAD < CHANNELS:
+                x_quantise(c + X_LEAD)
             c, rest = divmod(tick - 9, QUADS)
             if rest % 2 == 0:
                 if 0 <= c < CHANNELS:

@@ -17,12 +17,12 @@ BATCH, CHANNELS, OUTS = 128, 64, 512
 SPACE = 1024
 FLOPS = 2 * BATCH * OUTS * CHANNELS * SPACE
 
-GROUPS = 8
-QUADS = 4
-STEPS = CHANNELS * QUADS
+BLOCKS = 4
+STEPS = CHANNELS * BLOCKS
 X_LEAD = 8
 X_CHUNK = 4
-N_SCALAR = 170
+N_SCALAR = 142
+SCALAR_COLS = 256
 KICK_EVERY = 32
 KICK_PASSES = 2
 
@@ -36,10 +36,10 @@ def tile_gaussianspatialxfeaturelinear_kernel(tc, x, cx, cy, sigma, features, bi
     x_flat = x.rearrange("b c w h -> b (c w h)")
     with ExitStack() as ctx:
         const = ctx.enter_context(tc.tile_pool(name="const", bufs=1))
-        arg_pool = ctx.enter_context(tc.tile_pool(name="arg", bufs=4))
         x_pool = ctx.enter_context(tc.tile_pool(name="x", bufs=4))
         prod_pool = ctx.enter_context(tc.tile_pool(name="prod", bufs=10))
-        w_pool = ctx.enter_context(tc.tile_pool(name="w", bufs=8))
+        w_pool = ctx.enter_context(tc.tile_pool(name="w", bufs=4))
+        wq_pool = ctx.enter_context(tc.tile_pool(name="wq", bufs=8))
         xg_pool = ctx.enter_context(tc.tile_pool(name="xg", bufs=2))
         xq_pool = ctx.enter_context(tc.tile_pool(name="xq", bufs=4))
         ring = ctx.enter_context(tc.psum_pool(name="ring", bufs=6))
@@ -47,25 +47,10 @@ def tile_gaussianspatialxfeaturelinear_kernel(tc, x, cx, cy, sigma, features, bi
         acc_pool = ctx.enter_context(tc.psum_pool(name="acc", bufs=1))
         ctx.enter_context(tc.manual_schedule())
 
-        part_i = const.tile([P, 1], I32)
-        grid_i = const.tile([P, 48], I32)
-        ident_bf = const.tile([P, P], BF16)
-        ident_f = const.tile([P, P], F32)
-        nc.gpsimd.iota(part_i[:], pattern=[[0, 1]], base=0, channel_multiplier=1)
-        nc.gpsimd.iota(grid_i[:, 0:32], pattern=[[1, 32]], base=0, channel_multiplier=0)
-        nc.gpsimd.iota(grid_i[:, 32:48], pattern=[[2, 16]], base=0, channel_multiplier=0)
-        make_identity(nc, ident_bf[:])
-        make_identity(nc, ident_f[:])
-
-        raw = const.tile([P, 64 + 16 * CHANNELS], BF16)
-        raw_i = raw[:].bitcast(I32)
-        nc.vector.memset(raw_i[32:64, :], 0)
-        nc.vector.memset(raw_i[64:128, :], 0)
-        nc.vector.memset(raw_i[0:32, 24:32], 0)
-        nc.sync.dma_start(out=raw[0:32, 0:16], in_=cx.rearrange("(l g) a b c -> l (g a b c)", g=16))
-        nc.sync.dma_start(out=raw[0:32, 16:32], in_=cy.rearrange("(l g) a b c -> l (g a b c)", g=16))
-        nc.sync.dma_start(out=raw[0:32, 32:48], in_=sigma.rearrange("(l g) a b c -> l (g a b c)", g=16))
-        nc.sync.dma_start(out=raw[0:32, 64:], in_=features.rearrange("(l g) c a b -> l (g c a b)", g=16))
+        par = const.tile([P, 3, 16], BF16)
+        feat_bf = const.tile([P, BLOCKS * CHANNELS], BF16)
+        for v, vec in enumerate((cx, cy, sigma)):
+            nc.sync.dma_start(out=par[:, v, 0:BLOCKS], in_=vec.rearrange("(l g) a b c -> l (g a b c)", g=BLOCKS))
 
         x_tiles = {}
 
@@ -74,46 +59,62 @@ def tile_gaussianspatialxfeaturelinear_kernel(tc, x, cx, cy, sigma, features, bi
             nc.sync.dma_start(out=x_sb[:], in_=x_flat[:, j * X_CHUNK * SPACE : (j + 1) * X_CHUNK * SPACE])
             x_tiles[j] = x_sb
 
-        for j in range(4):
+        x_load(0)
+        nc.sync.dma_start(out=feat_bf[:], in_=features.rearrange("(l g) c a b -> l (g c a b)", g=BLOCKS))
+        for j in range(1, 4):
             x_load(j)
         bias_sb = const.tile([P, OUTS], BF16)
         nc.sync.dma_start(out=bias_sb[:], in_=bias.partition_broadcast(P))
+
+        grid_i = const.tile([P, 32], I32)
+        ident_f = const.tile([P, P], F32)
+        nc.gpsimd.iota(grid_i[:], pattern=[[1, 32]], base=0, channel_multiplier=0)
+        make_identity(nc, ident_f[:])
 
         warm = const.tile([P, 1], F32)
         nc.vector.memset(warm[:], 0.0)
         nc.scalar.activation(out=warm[:], in_=warm[:], func=ACT.Exp)
 
-        bit_i = const.tile([P, 1], I32)
-        nc.vector.tensor_scalar(out=bit_i[:], in0=part_i[:], scalar1=1, scalar2=None, op0=ALU.bitwise_and)
-        off = const.tile([P, 1], F32)
-        nc.vector.tensor_scalar(out=off[:], in0=bit_i[:], scalar1=-1.0, scalar2=15.5, op0=ALU.mult, op1=ALU.add)
-        grid = const.tile([P, 48], F32)
-        nc.vector.tensor_copy(out=grid[:], in_=grid_i[:])
-        spread = const.tile([P, 2, P], BF16)
-        nc.vector.memset(spread[:].rearrange("p h r -> p (h r)").bitcast(I32), 0)
-        for h in range(2):
-            nc.vector.tensor_copy(
-                out=spread[:, h, :].rearrange("p (l k e) -> p l k e", l=32, k=2, e=2)[:, :, h, :],
-                in_=ident_bf[:, 0:32].unsqueeze(2).to_broadcast([P, 32, 2]),
-            )
+        grid = const.tile([P, 32], F32)
+        nc.vector.tensor_scalar(out=grid[:], in0=grid_i[:], scalar1=-15.5, scalar2=None, op0=ALU.add)
 
-        par_ps = ring.tile([P, 4 * GROUPS], F32, tag="bank")
-        feat_ps = ring.tile([P, 512], F32, tag="bank")
-        raw_par = raw[:, 0:64].rearrange("p (v k g) -> p v k g", v=4, k=2, g=GROUPS)
-        for h in range(2):
-            nc.tensor.matmul(out=par_ps[:], lhsT=spread[:, h, :], rhs=raw_par[:, :, h, :], start=(h == 0), stop=(h == 1))
-        for h in range(2):
-            nc.tensor.matmul(
-                out=feat_ps[:],
-                lhsT=spread[:, h, :],
-                rhs=raw[:, 64 + 512 * h : 576 + 512 * h],
-                start=(h == 0),
-                stop=(h == 1),
+        inv = const.tile([P, BLOCKS], F32)
+        nc.vector.tensor_tensor(out=inv[:], in0=par[:, 2, 0:BLOCKS], in1=par[:, 2, 0:BLOCKS], op=ALU.mult)
+        nc.vector.reciprocal(out=inv[:], in_=inv[:])
+        dist = const.tile([P, 2, BLOCKS, 32], F32)
+        for v in range(2):
+            nc.vector.tensor_tensor(
+                out=dist[:, v],
+                in0=par[:, v, 0:BLOCKS].unsqueeze(2).to_broadcast([P, BLOCKS, 32]),
+                in1=grid[:].unsqueeze(1).to_broadcast([P, BLOCKS, 32]),
+                op=ALU.subtract,
             )
-        par = const.tile([P, 4, GROUPS], F32)
-        nc.vector.tensor_copy(out=par[:].rearrange("p v g -> p (v g)"), in_=par_ps[:])
-        feat = const.tile([P, GROUPS, CHANNELS], F32)
-        nc.scalar.copy(out=feat[:].rearrange("p g c -> p (g c)"), in_=feat_ps[:])
+        nc.vector.tensor_tensor(out=dist[:], in0=dist[:], in1=dist[:], op=ALU.mult)
+        for v in range(2):
+            nc.vector.tensor_tensor(
+                out=dist[:, v], in0=dist[:, v], in1=inv[:].unsqueeze(2).to_broadcast([P, BLOCKS, 32]), op=ALU.mult
+            )
+        factor = const.tile([P, 2, BLOCKS, 32], F32)
+        nc.scalar.activation(
+            out=factor[:].rearrange("p v g n -> p (v g n)"),
+            in_=dist[:].rearrange("p v g n -> p (v g n)"),
+            func=ACT.Exp,
+            scale=-1.0,
+        )
+        feat = const.tile([P, BLOCKS, CHANNELS], F32)
+        nc.scalar.copy(out=feat[:].rearrange("p g c -> p (g c)"), in_=feat_bf[:])
+
+        gauss = []
+
+        def gaussian(b):
+            gauss_b = const.tile([P, SPACE], F32, name="gauss%d" % b)
+            nc.vector.tensor_tensor(
+                out=gauss_b[:].rearrange("p (i j) -> p i j", i=32),
+                in0=factor[:, 0, b, :].unsqueeze(2).to_broadcast([P, 32, 32]),
+                in1=factor[:, 1, b, :].unsqueeze(1).to_broadcast([P, 32, 32]),
+                op=ALU.mult,
+            )
+            gauss.append(gauss_b)
 
         x_banks = {}
         xg_tiles = {}
@@ -152,56 +153,11 @@ def tile_gaussianspatialxfeaturelinear_kernel(tc, x, cx, cy, sigma, features, bi
                 in_=xg_tiles[j][:, i * SPACE : (i + 1) * SPACE],
             )
 
-        for c in range(4):
+        for c in range(X_LEAD):
             x_transposes(c)
             x_evacuate(c)
-        x_load(4)
-
-        ctr = const.tile([P, 2, GROUPS], F32)
-        nc.vector.tensor_scalar(out=ctr[:, 0, :], in0=par[:, 0, :], scalar1=15.5, scalar2=None, op0=ALU.add)
-        nc.vector.tensor_scalar(out=ctr[:, 1, :], in0=par[:, 1, :], scalar1=off[:], scalar2=None, op0=ALU.add)
-        inv = const.tile([P, GROUPS], F32)
-        nc.vector.tensor_tensor(out=inv[:], in0=par[:, 2, :], in1=par[:, 2, :], op=ALU.mult)
-        nc.vector.reciprocal(out=inv[:], in_=inv[:])
-        dist = const.tile([P, GROUPS, 48], F32)
-        nc.vector.tensor_tensor(
-            out=dist[:, :, 0:32],
-            in0=ctr[:, 0, :].unsqueeze(2).to_broadcast([P, GROUPS, 32]),
-            in1=grid[:, 0:32].unsqueeze(1).to_broadcast([P, GROUPS, 32]),
-            op=ALU.subtract,
-        )
-        nc.vector.tensor_tensor(
-            out=dist[:, :, 32:48],
-            in0=ctr[:, 1, :].unsqueeze(2).to_broadcast([P, GROUPS, 16]),
-            in1=grid[:, 32:48].unsqueeze(1).to_broadcast([P, GROUPS, 16]),
-            op=ALU.subtract,
-        )
-        nc.vector.tensor_tensor(out=dist[:], in0=dist[:], in1=dist[:], op=ALU.mult)
-        nc.vector.tensor_tensor(
-            out=dist[:], in0=dist[:], in1=inv[:].unsqueeze(2).to_broadcast([P, GROUPS, 48]), op=ALU.mult
-        )
-        gauss = []
-        for q in range(QUADS):
-            arg = arg_pool.tile([P, 2, 32, 16], F32)
-            nc.vector.tensor_tensor(
-                out=arg[:],
-                in0=dist[:, 2 * q : 2 * q + 2, 0:32].unsqueeze(3).to_broadcast([P, 2, 32, 16]),
-                in1=dist[:, 2 * q : 2 * q + 2, 32:48].unsqueeze(2).to_broadcast([P, 2, 32, 16]),
-                op=ALU.add,
-            )
-            gauss_q = const.tile([P, 2, 512], F32, name="gauss%d" % q)
-            nc.scalar.activation(
-                out=gauss_q[:].rearrange("p a k -> p (a k)"),
-                in_=arg[:].rearrange("p a i j -> p (a i j)"),
-                func=ACT.Exp,
-                scale=-1.0,
-            )
-            gauss.append(gauss_q)
-
-        for c in range(4, X_LEAD):
-            x_transposes(c)
-            x_evacuate(c)
-        x_load(5)
+            if c % X_CHUNK == X_CHUNK - 1:
+                x_load(c // X_CHUNK + 4)
 
         prods = {}
         w_banks = {}
@@ -211,61 +167,52 @@ def tile_gaussianspatialxfeaturelinear_kernel(tc, x, cx, cy, sigma, features, bi
 
         def product_tile(step):
             if step not in prods:
-                prod = prod_pool.tile([P, 2, 512], BF16)
+                prod = prod_pool.tile([P, SPACE], BF16)
                 prods[step] = prod
             return prods[step]
 
         def products(step, on_scalar):
-            c, q = divmod(step, QUADS)
-            n_scalar = scalar_share(step)
+            c, b = divmod(step, BLOCKS)
+            width = SPACE - scalar_share(step) * SCALAR_COLS
             prod = product_tile(step)
-            for a in range(2):
-                scale = feat[:, 2 * q + a, c : c + 1]
-                shared = a == 1 and n_scalar == 1
-                if on_scalar and shared:
-                    nc.scalar.activation(
-                        out=prod[:, a, 256:512], in_=gauss[q][:, a, 256:512], func=ACT.Copy, scale=scale
-                    )
-                if not on_scalar:
-                    width = 256 if shared else 512
-                    nc.vector.tensor_scalar(
-                        out=prod[:, a, 0:width], in0=gauss[q][:, a, 0:width], scalar1=scale, scalar2=None, op0=ALU.mult
-                    )
+            scale = feat[:, b, c : c + 1]
+            if on_scalar and width < SPACE:
+                nc.scalar.activation(out=prod[:, width:], in_=gauss[b][:, width:], func=ACT.Copy, scale=scale)
+            if not on_scalar:
+                nc.vector.tensor_scalar(
+                    out=prod[:, 0:width], in0=gauss[b][:, 0:width], scalar1=scale, scalar2=None, op0=ALU.mult
+                )
 
         def w_transposes(step):
-            for g in range(2):
-                w_ps = ring.tile([P, 2, 64, 2, 2], BF16, tag="bank")
-                for a in range(2):
-                    for u in range(2):
-                        nc.tensor.transpose(
-                            out=w_ps[:, a, :, u, :],
-                            in_=prods[step][:, a, (2 * g + u) * P : (2 * g + u + 1) * P],
-                            identity=ident_bf[:],
-                        )
-                w_banks[(step, g)] = w_ps
+            words = prods[step][:].bitcast(F32)
+            w_ps = ring.tile([P, 512], F32, tag="bank")
+            for v in range(4):
+                cols = slice(v * P, (v + 1) * P)
+                nc.tensor.transpose(out=w_ps[:, cols], in_=words[:, cols], identity=ident_f[:])
+            w_banks[step] = w_ps
 
         def w_evacuate(step):
-            c, q = divmod(step, QUADS)
-            for g in range(2):
-                if q == 0:
-                    wg = w_pool.tile([P, 4 * OUTS], BF16, align_bytes=64)
-                    wg_tiles[(c, g)] = wg
-                nc.scalar.copy(
-                    out=wg_tiles[(c, g)][:, 512 * q : 512 * (q + 1)],
-                    in_=w_banks[(step, g)][:].rearrange("p a l u e -> p (a l u e)"),
-                )
+            c, b = divmod(step, BLOCKS)
+            if b == 0:
+                wg = w_pool.tile([P, 2 * 4 * OUTS], BF16, align_bytes=64)
+                wg_tiles[c] = wg
+            dst = wg_tiles[c][:].bitcast(F32).rearrange("p (g b l u) -> p g b l u", g=2, b=BLOCKS, l=P, u=2)
+            nc.scalar.copy(
+                out=dst[:, :, b], in_=w_banks[step][:].rearrange("p (g u l) -> p g l u", g=2, u=2, l=P)
+            )
 
         def w_quantise(c, g, h):
             if h == 0:
-                w_codes = w_pool.tile([P, OUTS], U32, align_bytes=64)
-                w_scales = w_pool.tile([P, OUTS], U8, align_bytes=64)
+                w_codes = wq_pool.tile([P, OUTS], U32, align_bytes=64)
+                w_scales = wq_pool.tile([P, OUTS], U8, align_bytes=64)
                 wq_tiles[(c, g)] = (w_codes, w_scales)
             codes, scales = wq_tiles[(c, g)]
             words = slice(h * 256, (h + 1) * 256)
+            first = (g * OUTS + h * 256) * 4
             nc.vector.quantize_mx(
                 out=codes[:, words].bitcast(FP8X4),
                 scales=scales[:, words],
-                in_=wg_tiles[(c, g)][:, h * 1024 : (h + 1) * 1024],
+                in_=wg_tiles[c][:, first : first + 1024],
             )
 
         def mx_pass(c, g):
@@ -295,13 +242,16 @@ def tile_gaussianspatialxfeaturelinear_kernel(tc, x, cx, cy, sigma, features, bi
                 stop=True,
             )
 
+        gaussian(0)
         products(0, True)
         n_passes = 0
         for tick in range(STEPS + 16):
-            if tick + 1 < STEPS:
-                products(tick + 1, True)
             if tick < STEPS:
                 products(tick, False)
+            if tick + 1 < BLOCKS:
+                gaussian(tick + 1)
+            if tick + 1 < STEPS:
+                products(tick + 1, True)
             if tick < X_LEAD:
                 x_quantise(tick)
             step = tick - 1
@@ -310,24 +260,24 @@ def tile_gaussianspatialxfeaturelinear_kernel(tc, x, cx, cy, sigma, features, bi
                     idle_pass(xq_tiles[0], xq_tiles[0])
             if 0 <= step < STEPS:
                 w_transposes(step)
-                c = step // QUADS - 1 + X_LEAD
-                if step % QUADS == 0 and X_LEAD <= c < CHANNELS:
+                c = step // BLOCKS - 1 + X_LEAD
+                if step % BLOCKS == 0 and X_LEAD <= c < CHANNELS:
                     x_transposes(c)
                     if c % X_CHUNK == 3 and c // X_CHUNK + 4 < CHANNELS // X_CHUNK:
                         x_load(c // X_CHUNK + 4)
             step = tick - 2
             if 0 <= step < STEPS:
                 w_evacuate(step)
-                c = step // QUADS - 1 + X_LEAD
-                if step % QUADS == 0 and X_LEAD <= c < CHANNELS:
+                c = step // BLOCKS - 1 + X_LEAD
+                if step % BLOCKS == 0 and X_LEAD <= c < CHANNELS:
                     x_evacuate(c)
-            c, piece = divmod(tick - 5, QUADS)
+            c, piece = divmod(tick - 5, BLOCKS)
             if 0 <= c < CHANNELS:
                 w_quantise(c, piece % 2, piece // 2)
-            c, rest = divmod(tick - 8, QUADS)
+            c, rest = divmod(tick - 8, BLOCKS)
             if rest == 0 and c >= 0 and c + X_LEAD < CHANNELS:
                 x_quantise(c + X_LEAD)
-            c, rest = divmod(tick - 9, QUADS)
+            c, rest = divmod(tick - 9, BLOCKS)
             if rest % 2 == 0:
                 if 0 <= c < CHANNELS:
                     mx_pass(c, rest // 2)
@@ -340,9 +290,9 @@ def tile_gaussianspatialxfeaturelinear_kernel(tc, x, cx, cy, sigma, features, bi
 
         res = const.tile([P, OUTS], F32)
         nc.vector.tensor_tensor(
-            out=res[:].rearrange("b (l g) -> b l g", g=GROUPS),
-            in0=acc[:].rearrange("b (g l) -> b l g", g=GROUPS),
-            in1=bias_sb[:].rearrange("b (l g) -> b l g", g=GROUPS),
+            out=res[:].rearrange("b (l g) -> b l g", g=BLOCKS),
+            in0=acc[:].rearrange("b (g l) -> b l g", g=BLOCKS),
+            in1=bias_sb[:].rearrange("b (l g) -> b l g", g=BLOCKS),
             op=ALU.add,
         )
         nc.sync.dma_start(out=out, in_=res[:])

@@ -186,9 +186,10 @@ def tile_gaussianspatialxfeaturelinear_kernel(tc, x, cx, cy, sigma, features, bi
         def w_transposes(step):
             words = prods[step][:].bitcast(F32)
             w_ps = ring.tile([P, 512], F32, tag="bank")
+            turned = w_ps[:].rearrange("p (g l u) -> p g l u", g=2, l=P, u=2)
             for v in range(4):
                 cols = slice(v * P, (v + 1) * P)
-                nc.tensor.transpose(out=w_ps[:, cols], in_=words[:, cols], identity=ident_f[:])
+                nc.tensor.transpose(out=turned[:, v // 2, :, v % 2], in_=words[:, cols], identity=ident_f[:])
             w_banks[step] = w_ps
 
         def w_evacuate(step):
@@ -196,10 +197,8 @@ def tile_gaussianspatialxfeaturelinear_kernel(tc, x, cx, cy, sigma, features, bi
             if b == 0:
                 wg = w_pool.tile([P, 2 * 4 * OUTS], BF16, align_bytes=64)
                 wg_tiles[c] = wg
-            dst = wg_tiles[c][:].bitcast(F32).rearrange("p (g b l u) -> p g b l u", g=2, b=BLOCKS, l=P, u=2)
-            nc.scalar.copy(
-                out=dst[:, :, b], in_=w_banks[step][:].rearrange("p (g u l) -> p g l u", g=2, u=2, l=P)
-            )
+            dst = wg_tiles[c][:].bitcast(F32).rearrange("p (g b n) -> p g b n", g=2, b=BLOCKS)
+            nc.scalar.copy(out=dst[:, :, b], in_=w_banks[step][:].rearrange("p (g n) -> p g n", g=2))
 
         def w_quantise(c, g, h):
             if h == 0:

from contextlib import ExitStack

import concourse.mybir as mybir
from concourse.masks import make_identity

F32 = mybir.dt.float32
BF16 = mybir.dt.bfloat16
I32 = mybir.dt.int32
U32 = mybir.dt.uint32
U8 = mybir.dt.uint8
FP8X4 = mybir.dt.float8_e4m3fn_x4
ALU = mybir.AluOpType
ACT = mybir.ActivationFunctionType

P = 128
BATCH, CHANNELS, OUTS = 128, 64, 512
SPACE = 1024
FLOPS = 2 * BATCH * OUTS * CHANNELS * SPACE

BLOCKS = 4
STEPS = CHANNELS * BLOCKS
X_LEAD = 8
X_CHUNK = 4
N_SCALAR = 142
SCALAR_COLS = 256
KICK_EVERY = 32
KICK_PASSES = 2


def scalar_share(step):
    return ((step + 1) * N_SCALAR) // STEPS - (step * N_SCALAR) // STEPS


def tile_gaussianspatialxfeaturelinear_kernel(tc, x, cx, cy, sigma, features, bias, out):
    nc = tc.nc
    x_flat = x.rearrange("b c w h -> b (c w h)")
    with ExitStack() as ctx:
        const = ctx.enter_context(tc.tile_pool(name="const", bufs=1))
        x_pool = ctx.enter_context(tc.tile_pool(name="x", bufs=4))
        prod_pool = ctx.enter_context(tc.tile_pool(name="prod", bufs=10))
        w_pool = ctx.enter_context(tc.tile_pool(name="w", bufs=4))
        wq_pool = ctx.enter_context(tc.tile_pool(name="wq", bufs=8))
        xg_pool = ctx.enter_context(tc.tile_pool(name="xg", bufs=2))
        xq_pool = ctx.enter_context(tc.tile_pool(name="xq", bufs=4))
        ring = ctx.enter_context(tc.psum_pool(name="ring", bufs=6))
        idle_pool = ctx.enter_context(tc.psum_pool(name="idle", bufs=1))
        acc_pool = ctx.enter_context(tc.psum_pool(name="acc", bufs=1))
        ctx.enter_context(tc.manual_schedule())

        par = const.tile([P, 3, 16], BF16)
        feat_bf = const.tile([P, BLOCKS * CHANNELS], BF16)
        for v, vec in enumerate((cx, cy, sigma)):
            nc.sync.dma_start(out=par[:, v, 0:BLOCKS], in_=vec.rearrange("(l g) a b c -> l (g a b c)", g=BLOCKS))

        x_tiles = {}

        def x_load(j):
            x_sb = x_pool.tile([P, X_CHUNK * SPACE], BF16)
            nc.sync.dma_start(out=x_sb[:], in_=x_flat[:, j * X_CHUNK * SPACE : (j + 1) * X_CHUNK * SPACE])
            x_tiles[j] = x_sb

        x_load(0)
        nc.sync.dma_start(out=feat_bf[:], in_=features.rearrange("(l g) c a b -> l (g c a b)", g=BLOCKS))
        for j in range(1, 4):
            x_load(j)
        bias_sb = const.tile([P, OUTS], BF16)
        nc.sync.dma_start(out=bias_sb[:], in_=bias.partition_broadcast(P))

        grid_i = const.tile([P, 32], I32)
        ident_f = const.tile([P, P], F32)
        nc.gpsimd.iota(grid_i[:], pattern=[[1, 32]], base=0, channel_multiplier=0)
        make_identity(nc, ident_f[:])

        warm = const.tile([P, 1], F32)
        nc.vector.memset(warm[:], 0.0)
        nc.scalar.activation(out=warm[:], in_=warm[:], func=ACT.Exp)

        grid = const.tile([P, 32], F32)
        nc.vector.tensor_scalar(out=grid[:], in0=grid_i[:], scalar1=-15.5, scalar2=None, op0=ALU.add)

        inv = const.tile([P, BLOCKS], F32)
        nc.vector.tensor_tensor(out=inv[:], in0=par[:, 2, 0:BLOCKS], in1=par[:, 2, 0:BLOCKS], op=ALU.mult)
        nc.vector.reciprocal(out=inv[:], in_=inv[:])
        dist = const.tile([P, 2, BLOCKS, 32], F32)
        for v in range(2):
            nc.vector.tensor_tensor(
                out=dist[:, v],
                in0=par[:, v, 0:BLOCKS].unsqueeze(2).to_broadcast([P, BLOCKS, 32]),
                in1=grid[:].unsqueeze(1).to_broadcast([P, BLOCKS, 32]),
                op=ALU.subtract,
            )
        nc.vector.tensor_tensor(out=dist[:], in0=dist[:], in1=dist[:], op=ALU.mult)
        for v in range(2):
            nc.vector.tensor_tensor(
                out=dist[:, v], in0=dist[:, v], in1=inv[:].unsqueeze(2).to_broadcast([P, BLOCKS, 32]), op=ALU.mult
            )
        factor = const.tile([P, 2, BLOCKS, 32], F32)
        nc.scalar.activation(
            out=factor[:].rearrange("p v g n -> p (v g n)"),
            in_=dist[:].rearrange("p v g n -> p (v g n)"),
            func=ACT.Exp,
            scale=-1.0,
        )
        feat = const.tile([P, BLOCKS, CHANNELS], F32)
        nc.scalar.copy(out=feat[:].rearrange("p g c -> p (g c)"), in_=feat_bf[:])

        gauss = []

        def gaussian(b):
            gauss_b = const.tile([P, SPACE], F32, name="gauss%d" % b)
            nc.vector.tensor_tensor(
                out=gauss_b[:].rearrange("p (i j) -> p i j", i=32),
                in0=factor[:, 0, b, :].unsqueeze(2).to_broadcast([P, 32, 32]),
                in1=factor[:, 1, b, :].unsqueeze(1).to_broadcast([P, 32, 32]),
                op=ALU.mult,
            )
            gauss.append(gauss_b)

        x_banks = {}
        xg_tiles = {}
        xq_tiles = {}

        def x_transposes(c):
            words = x_tiles[c // X_CHUNK][:].bitcast(F32)
            x_ps = ring.tile([P, 512], F32, tag="bank")
            for v in range(4):
                col = (c % X_CHUNK) * 512 + v * P
                nc.tensor.transpose(out=x_ps[:, v * P : (v + 1) * P], in_=words[:, col : col + P], identity=ident_f[:])
            x_banks[c] = x_ps

        def x_evacuate(c):
            if c % X_CHUNK == 0:
                xg = xg_pool.tile([P, X_CHUNK * SPACE], BF16, align_bytes=64)
                xg_tiles[c // X_CHUNK] = xg
            dst = xg_tiles[c // X_CHUNK][:].bitcast(F32).rearrange(
                "p (c g b u) -> p c g b u", c=X_CHUNK, g=2, b=BATCH, u=2
            )
            nc.scalar.copy(
                out=dst[:, c % X_CHUNK], in_=x_banks[c][:].rearrange("p (g u b) -> p g b u", g=2, u=2, b=BATCH)
            )

        def x_quantise(c):
            j, i = divmod(c, X_CHUNK)
            if i == 0:
                x_codes = xq_pool.tile([P, X_CHUNK * 2 * BATCH], U32, align_bytes=64)
                x_scales = xq_pool.tile([P, X_CHUNK * 2 * BATCH], U8, align_bytes=64)
                xq_tiles[j] = (x_codes, x_scales)
            codes, scales = xq_tiles[j]
            words = slice(i * 2 * BATCH, (i + 1) * 2 * BATCH)
            nc.vector.quantize_mx(
                out=codes[:, words].bitcast(FP8X4),
                scales=scales[:, words],
                in_=xg_tiles[j][:, i * SPACE : (i + 1) * SPACE],
            )

        for c in range(X_LEAD):
            x_transposes(c)
            x_evacuate(c)
            if c % X_CHUNK == X_CHUNK - 1:
                x_load(c // X_CHUNK + 4)

        prods = {}
        w_banks = {}
        wg_tiles = {}
        wq_tiles = {}
        acc = acc_pool.tile([P, OUTS], F32)

        def product_tile(step):
            if step not in prods:
                prod = prod_pool.tile([P, SPACE], BF16)
                prods[step] = prod
            return prods[step]

        def products(step, on_scalar):
            c, b = divmod(step, BLOCKS)
            width = SPACE - scalar_share(step) * SCALAR_COLS
            prod = product_tile(step)
            scale = feat[:, b, c : c + 1]
            if on_scalar and width < SPACE:
                nc.scalar.activation(out=prod[:, width:], in_=gauss[b][:, width:], func=ACT.Copy, scale=scale)
            if not on_scalar:
                nc.vector.tensor_scalar(
                    out=prod[:, 0:width], in0=gauss[b][:, 0:width], scalar1=scale, scalar2=None, op0=ALU.mult
                )

        def w_transposes(step):
            words = prods[step][:].bitcast(F32)
            w_ps = ring.tile([P, 512], F32, tag="bank")
            turned = w_ps[:].rearrange("p (g l u) -> p g l u", g=2, l=P, u=2)
            for v in range(4):
                cols = slice(v * P, (v + 1) * P)
                nc.tensor.transpose(out=turned[:, v // 2, :, v % 2], in_=words[:, cols], identity=ident_f[:])
            w_banks[step] = w_ps

        def w_evacuate(step):
            c, b = divmod(step, BLOCKS)
            if b == 0:
                wg = w_pool.tile([P, 2 * 4 * OUTS], BF16, align_bytes=64)
                wg_tiles[c] = wg
            dst = wg_tiles[c][:].bitcast(F32).rearrange("p (g b n) -> p g b n", g=2, b=BLOCKS)
            nc.scalar.copy(out=dst[:, :, b], in_=w_banks[step][:].rearrange("p (g n) -> p g n", g=2))

        def w_quantise(c, g, h):
            if h == 0:
                w_codes = wq_pool.tile([P, OUTS], U32, align_bytes=64)
                w_scales = wq_pool.tile([P, OUTS], U8, align_bytes=64)
                wq_tiles[(c, g)] = (w_codes, w_scales)
            codes, scales = wq_tiles[(c, g)]
            words = slice(h * 256, (h + 1) * 256)
            first = (g * OUTS + h * 256) * 4
            nc.vector.quantize_mx(
                out=codes[:, words].bitcast(FP8X4),
                scales=scales[:, words],
                in_=wg_tiles[c][:, first : first + 1024],
            )

        def mx_pass(c, g):
            x_codes, x_scales = xq_tiles[c // X_CHUNK]
            w_codes, w_scales = wq_tiles[(c, g)]
            cols = slice(((c % X_CHUNK) * 2 + g) * BATCH, ((c % X_CHUNK) * 2 + g + 1) * BATCH)
            nc.tensor.matmul_mx(
                out=acc[:],
                lhsT=x_codes[:, cols].bitcast(FP8X4),
                lhsT_scale=x_scales[:, cols],
                rhs=w_codes[:].bitcast(FP8X4),
                rhs_scale=w_scales[:],
                start=(c == 0 and g == 0),
                stop=(c == CHANNELS - 1 and g == 1),
            )

        idle = idle_pool.tile([P, OUTS], F32)

        def idle_pass(stationary, moving):
            nc.tensor.matmul_mx(
                out=idle[:],
                lhsT=stationary[0][:, 0:BATCH].bitcast(FP8X4),
                lhsT_scale=stationary[1][:, 0:BATCH],
                rhs=moving[0][:, 0:OUTS].bitcast(FP8X4),
                rhs_scale=moving[1][:, 0:OUTS],
                start=True,
                stop=True,
            )

        gaussian(0)
        products(0, True)
        n_passes = 0
        for tick in range(STEPS + 16):
            if tick < STEPS:
                products(tick, False)
            if tick + 1 < BLOCKS:
                gaussian(tick + 1)
            if tick + 1 < STEPS:
                products(tick + 1, True)
            if tick < X_LEAD:
                x_quantise(tick)
            step = tick - 1
            if step == 0:
                for i in range(3):
                    idle_pass(xq_tiles[0], xq_tiles[0])
            if 0 <= step < STEPS:
                w_transposes(step)
                c = step // BLOCKS - 1 + X_LEAD
                if step % BLOCKS == 0 and X_LEAD <= c < CHANNELS:
                    x_transposes(c)
                    if c % X_CHUNK == 3 and c // X_CHUNK + 4 < CHANNELS // X_CHUNK:
                        x_load(c // X_CHUNK + 4)
            step = tick - 2
            if 0 <= step < STEPS:
                w_evacuate(step)
                c = step // BLOCKS - 1 + X_LEAD
                if step % BLOCKS == 0 and X_LEAD <= c < CHANNELS:
                    x_evacuate(c)
            c, piece = divmod(tick - 5, BLOCKS)
            if 0 <= c < CHANNELS:
                w_quantise(c, piece % 2, piece // 2)
            c, rest = divmod(tick - 8, BLOCKS)
            if rest == 0 and c >= 0 and c + X_LEAD < CHANNELS:
                x_quantise(c + X_LEAD)
            c, rest = divmod(tick - 9, BLOCKS)
            if rest % 2 == 0:
                if 0 <= c < CHANNELS:
                    mx_pass(c, rest // 2)
                    n_passes += 1
                    if n_passes % KICK_EVERY == 0 and n_passes < 2 * CHANNELS:
                        for i in range(KICK_PASSES):
                            idle_pass(xq_tiles[c // X_CHUNK], wq_tiles[(c, rest // 2)])
                elif c < 0 and tick >= 3:
                    idle_pass(xq_tiles[0], xq_tiles[0])

        res = const.tile([P, OUTS], F32)
        nc.vector.tensor_tensor(
            out=res[:].rearrange("b (l g) -> b l g", g=BLOCKS),
            in0=acc[:].rearrange("b (g l) -> b l g", g=BLOCKS),
            in1=bias_sb[:].rearrange("b (l g) -> b l g", g=BLOCKS),
            op=ALU.add,
        )
        nc.sync.dma_start(out=out, in_=res[:])
